import numpy as np
import ml_dtypes


def mxq(x, axis, fmt="e4m3"):
    dtype, down = {"e4m3": (ml_dtypes.float8_e4m3fn, 7), "e5m2": (ml_dtypes.float8_e5m2, 14)}[fmt]
    v = np.moveaxis(np.asarray(x, np.float32).astype(ml_dtypes.bfloat16).astype(np.float64), axis, -1)
    blocks = v.reshape(v.shape[:-1] + (-1, 32))
    amax = np.abs(blocks).max(-1, keepdims=True)
    byte = np.maximum(np.where(amax > 0, np.frexp(amax)[1] - 1 + 127, 0) - down, 1)
    scale = np.exp2(byte - 127.0)
    codes = (blocks / scale).astype(np.float32).astype(dtype).astype(np.float64)
    return np.moveaxis((codes * scale).reshape(v.shape), -1, axis)


WIDE = False


def mx_kscale(k):
    if not WIDE:
        return np.ones(k)
    levels = np.array([10, -10, 5, -5, 0])
    a = np.random.permutation(np.resize(levels, k // 512 * 4)).reshape(k // 512, 4)
    idx = np.arange(k)
    return np.exp2(a[idx // 512, idx % 128 // 32])


BF16 = ml_dtypes.bfloat16


def bf(x):
    return np.asarray(x, np.float32).astype(BF16)


def f64(x):
    return np.asarray(x).astype(np.float64)


B, N, E, H, NOPE, VDIM, ROPE, QR, KVR = 2, 128, 512, 16, 32, 128, 32, 8192, 512
QH = NOPE + ROPE
BASE = 10000.0


def rope(v):
    d = v.shape[-1]
    n = v.shape[-2]
    theta = BASE ** (-2.0 * np.arange(d // 2) / d)
    ang = np.arange(n)[:, None] * theta[None, :]
    cos, sin = np.cos(ang), np.sin(ang)
    v1, v2 = v[..., 0::2], v[..., 1::2]
    return np.stack([v1 * cos - v2 * sin, v1 * sin + v2 * cos], axis=-1).reshape(v.shape)


def setup_inputs():
    s, t = mx_kscale(E), mx_kscale(QR)
    return {"x": bf(np.random.standard_normal((B, N, E)) * s),
            "Wqa": bf(np.random.standard_normal((E, QR)) / np.sqrt(E) / s[:, None] * t),
            "Wqb": bf(np.random.standard_normal((QR, H * QH)) / np.sqrt(QR) / t[:, None])}


def reference(x, Wqa, Wqb):
    cq = mxq(f64(x), 2, "e4m3") @ mxq(f64(Wqa), 0, "e4m3")
    q = mxq(cq, 2, "e4m3") @ mxq(f64(Wqb), 0, "e4m3")
    q = q.reshape(B, N, H, QH).transpose(0, 2, 1, 3)
    return np.concatenate([q[..., :NOPE], rope(q[..., NOPE:])], axis=-1)

@@ -1,0 +1,271 @@
+import math
+from contextlib import ExitStack
+
+import concourse.mybir as mybir
+from concourse.masks import make_identity
+
+F32 = mybir.dt.float32
+BF16 = mybir.dt.bfloat16
+U32 = mybir.dt.uint32
+U8 = mybir.dt.uint8
+FP8X4 = mybir.dt.float8_e4m3fn_x4
+ALU = mybir.AluOpType
+ACT = mybir.ActivationFunctionType
+
+B, N, E, H, NOPE, ROPE, QR = 2, 128, 512, 16, 32, 32, 8192
+QH = NOPE + ROPE
+HQ = H * QH
+BASE = 10000.0
+
+P = 128
+PACK = 4
+K_PASS = P * PACK
+BANK = 512
+
+N_GROUPS = QR // K_PASS
+SLAB = 1024
+GROUPS_PER_SLAB = SLAB // K_PASS
+HALVES = HQ // BANK
+HEADS_PER_HALF = BANK // QH
+PAIRS = ROPE // 2
+
+RUN = 4
+WQA_SCALAR_COLUMNS = 128
+RAW_BUFS = 12
+
+ROUND_MAGIC = 1.5 * 2.0**23
+
+FLOPS = 2 * B * N * E * QR + 2 * B * N * QR * HQ
+
+
+def tile_multilatentattention_pa_k_kernel(tc, x, Wqa, Wqb, out):
+    nc = tc.nc
+    with ExitStack() as ctx:
+        ctx.enter_context(tc.manual_schedule())
+        const = ctx.enter_context(tc.tile_pool(name="const", bufs=1))
+        raw = ctx.enter_context(tc.tile_pool(name="raw", bufs=RAW_BUFS))
+        work = ctx.enter_context(tc.tile_pool(name="work", bufs=3))
+        results = ctx.enter_context(tc.tile_pool(name="results", bufs=2))
+        cq_psum = ctx.enter_context(tc.psum_pool(name="cq_psum", bufs=4))
+        q_psum = ctx.enter_context(tc.psum_pool(name="q_psum", bufs=1))
+
+        def regroup(copy, grouped, rows):
+            copy(
+                out=grouped.rearrange("p (c i) t -> p c t i", i=RUN),
+                in_=rows.rearrange("p t (c i) -> p c t i", i=RUN),
+            )
+
+        def quantise(words, scales, grouped):
+            nc.vector.quantize_mx(
+                out=words.bitcast(FP8X4),
+                scales=scales,
+                in_=grouped.rearrange("p w t -> p (w t)"),
+            )
+
+        x_rows = const.tile([P, B, E], BF16)
+        nc.sync.dma_start(out=x_rows[:], in_=x.rearrange("b n e -> n b e"))
+
+        position = const.tile([P, 1], F32)
+        nc.gpsimd.iota(
+            position[:],
+            pattern=[[0, 1]],
+            base=0,
+            channel_multiplier=1,
+            allow_small_or_imprecise_dtypes=True,
+        )
+        identity = const.tile([P, P], F32)
+        make_identity(nc, identity[:])
+
+        turns = const.tile([P, PAIRS], F32)
+        nc.vector.tensor_scalar(
+            out=turns[:, 0:1], in0=position[:], scalar1=1.0 / (2.0 * math.pi), scalar2=None, op0=ALU.mult
+        )
+        ratio = BASE ** (-2.0 / ROPE)
+        filled = 1
+        while filled < PAIRS:
+            nc.vector.tensor_scalar(
+                out=turns[:, filled : 2 * filled],
+                in0=turns[:, 0:filled],
+                scalar1=ratio**filled,
+                scalar2=None,
+                op0=ALU.mult,
+            )
+            filled *= 2
+        COS = slice(0, ROPE)
+        MINUS_SIN = slice(ROPE, ROPE + PAIRS)
+        PLUS_SIN = slice(ROPE + PAIRS, ROPE + 2 * PAIRS)
+        phase = const.tile([P, ROPE + 2 * PAIRS], F32)
+        nc.vector.tensor_scalar(
+            out=phase[:, COS].rearrange("p (i e) -> p i e", e=2),
+            in0=turns[:].unsqueeze(2).to_broadcast([P, PAIRS, 2]),
+            scalar1=0.25,
+            scalar2=None,
+            op0=ALU.add,
+        )
+        nc.vector.tensor_scalar(
+            out=phase[:, MINUS_SIN], in0=turns[:], scalar1=-1.0, scalar2=None, op0=ALU.mult
+        )
+        nc.vector.tensor_copy(out=phase[:, PLUS_SIN], in_=turns[:])
+        whole = const.tile([P, ROPE + 2 * PAIRS], F32)
+        nc.vector.tensor_scalar(
+            out=whole[:],
+            in0=phase[:],
+            scalar1=ROUND_MAGIC,
+            scalar2=ROUND_MAGIC,
+            op0=ALU.add,
+            op1=ALU.subtract,
+        )
+        part = const.tile([P, ROPE + 2 * PAIRS], F32)
+        nc.vector.tensor_sub(out=part[:], in0=phase[:], in1=whole[:])
+        table = const.tile([P, ROPE + 2 * PAIRS], F32)
+        nc.scalar.activation(out=table[:], in_=part[:], func=ACT.Sin, scale=2.0 * math.pi)
+
+        x_pairs = x_rows[:].bitcast(F32).rearrange("n b (p u) -> n b u p", u=2)
+        x_turned = cq_psum.tile([P, PACK, P], F32, name="x_turned", tag="cq_bank")
+        for b in range(B):
+            for u in range(2):
+                nc.tensor.transpose(x_turned[:, 2 * b + u, :], x_pairs[:, b, u, :], identity[:])
+        x_grouped = const.tile([P, B * N, PACK], BF16, align_bytes=64)
+        nc.vector.tensor_copy(
+            out=x_grouped[:].bitcast(F32).rearrange("p (b n) u -> p b n u", b=B),
+            in_=x_turned[:].rearrange("p (b u) n -> p b n u", u=2),
+        )
+        x_words = const.tile([P, B * N], U32, align_bytes=64)
+        x_scales = const.tile([P, B * N], U8, align_bytes=64)
+        quantise(x_words[:], x_scales[:], x_grouped[:])
+
+        cq_words = const.tile([P, N_GROUPS, B * N], U32, align_bytes=64)
+        cq_scales = const.tile([P, N_GROUPS, B * N], U8, align_bytes=64)
+        q_sums = {}
+        for b in range(B):
+            for half in range(HALVES):
+                q_sums[(b, half)] = q_psum.tile(
+                    [P, BANK], F32, name="q_sums_%d_%d" % (b, half), tag="q_sums_%d_%d" % (b, half)
+                )
+        wqa_rows, wqa_grouped, wqa_words, wqa_scales = {}, {}, {}, {}
+        cq_banks, cq_grouped = {}, {}
+        wqb_grouped, wqb_words, wqb_scales = {}, {}, {}
+
+        def regroup_wqa(g):
+            slab, place = divmod(g, GROUPS_PER_SLAB)
+            if place == 0:
+                wqa_rows[slab] = raw.tile([P, PACK, SLAB], BF16, name="wqa_rows", tag="rows")
+                nc.sync.dma_start(
+                    out=wqa_rows[slab][:],
+                    in_=Wqa[:, slab * SLAB : (slab + 1) * SLAB].rearrange("(p t) w -> p t w", t=PACK),
+                )
+            rows = wqa_rows[slab][:, :, place * K_PASS : (place + 1) * K_PASS]
+            wqa_grouped[g] = work.tile(
+                [P, K_PASS, PACK], BF16, name="wqa_grouped", tag="wqa_grouped", align_bytes=64
+            )
+            cut = WQA_SCALAR_COLUMNS
+            regroup(nc.scalar.copy, wqa_grouped[g][:, 0:cut, :], rows[:, :, 0:cut])
+            regroup(nc.vector.tensor_copy, wqa_grouped[g][:, cut:K_PASS, :], rows[:, :, cut:K_PASS])
+
+        def quantise_wqa(g):
+            wqa_words[g] = work.tile([P, K_PASS], U32, name="wqa_words", tag="wqa_words", align_bytes=64)
+            wqa_scales[g] = work.tile([P, K_PASS], U8, name="wqa_scales", tag="wqa_scales", align_bytes=64)
+            quantise(wqa_words[g][:], wqa_scales[g][:], wqa_grouped[g][:])
+
+        def first_product(g):
+            for b in range(B):
+                cq_banks[(g, b)] = cq_psum.tile([P, PACK, N], F32, name="cq_bank", tag="cq_bank")
+                for t in range(PACK):
+                    nc.tensor.matmul_mx(
+                        out=cq_banks[(g, b)][:, t, :],
+                        lhsT=wqa_words[g][:, t * P : (t + 1) * P].bitcast(FP8X4),
+                        lhsT_scale=wqa_scales[g][:, t * P : (t + 1) * P],
+                        rhs=x_words[:, b * N : (b + 1) * N].bitcast(FP8X4),
+                        rhs_scale=x_scales[:, b * N : (b + 1) * N],
+                        start=True,
+                        stop=True,
+                    )
+
+        def round_cq(g):
+            cq_grouped[g] = work.tile(
+                [P, B * N, PACK], BF16, name="cq_grouped", tag="cq_grouped", align_bytes=64
+            )
+            for b in range(B):
+                nc.scalar.copy(
+                    out=cq_grouped[g][:, b * N : (b + 1) * N, :],
+                    in_=cq_banks[(g, b)][:].rearrange("p t n -> p n t"),
+                )
+
+        def quantise_cq(g):
+            quantise(cq_words[:, g, :], cq_scales[:, g, :], cq_grouped[g][:])
+
+        def regroup_wqb(g):
+            rows = raw.tile([P, PACK, HQ], BF16, name="wqb_rows", tag="rows")
+            nc.sync.dma_start(
+                out=rows[:],
+                in_=Wqb[g * K_PASS : (g + 1) * K_PASS, :].rearrange("(t p) w -> p t w", p=P),
+            )
+            for half, copy in enumerate((nc.scalar.copy, nc.vector.tensor_copy)):
+                wqb_grouped[(g, half)] = work.tile(
+                    [P, BANK, PACK],
+                    BF16,
+                    name="wqb_grouped_%d" % half,
+                    tag="wqb_grouped_%d" % half,
+                    align_bytes=64,
+                )
+                regroup(copy, wqb_grouped[(g, half)][:], rows[:, :, half * BANK : (half + 1) * BANK])
+
+        def second_product(g):
+            for half in range(HALVES):
+                wqb_words[half] = work.tile(
+                    [P, BANK], U32, name="wqb_words_%d" % half, tag="wqb_words_%d" % half, align_bytes=64
+                )
+                wqb_scales[half] = work.tile(
+                    [P, BANK], U8, name="wqb_scales_%d" % half, tag="wqb_scales_%d" % half, align_bytes=64
+                )
+                quantise(wqb_words[half][:], wqb_scales[half][:], wqb_grouped[(g, half)][:])
+                for b in range(B):
+                    nc.tensor.matmul_mx(
+                        out=q_sums[(b, half)][:],
+                        lhsT=cq_words[:, g, b * N : (b + 1) * N].bitcast(FP8X4),
+                        lhsT_scale=cq_scales[:, g, b * N : (b + 1) * N],
+                        rhs=wqb_words[half][:].bitcast(FP8X4),
+                        rhs_scale=wqb_scales[half][:],
+                        start=(g == 0),
+                        stop=(g == N_GROUPS - 1),
+                    )
+
+        def run(stage, g):
+            if 0 <= g < N_GROUPS:
+                stage(g)
+
+        for step in range(2 * N_GROUPS + 1):
+            run(regroup_wqa, step)
+            run(regroup_wqb, step - N_GROUPS)
+            run(quantise_wqa, step - 1)
+            run(first_product, step - 1)
+            run(round_cq, step - 2)
+            run(quantise_cq, step - 3)
+            run(second_product, step - N_GROUPS - 1)
+
+        def over_heads(part_of_table, width):
+            return table[:, part_of_table].unsqueeze(1).to_broadcast([P, HEADS_PER_HALF, width])
+
+        for half in range(HALVES):
+            for b in range(B):
+                q = q_sums[(b, half)][:].rearrange("p (h d) -> p h d", d=QH)
+                rotated = q[:, :, NOPE:QH]
+                pairs = rotated.rearrange("p h (i e) -> p h i e", e=2)
+                result = results.tile([P, HEADS_PER_HALF, QH], F32)
+                nc.scalar.copy(out=result[:, :, 0:NOPE], in_=q[:, :, 0:NOPE])
+                straight = results.tile([P, HEADS_PER_HALF, ROPE], F32)
+                nc.vector.tensor_mul(out=straight[:], in0=rotated, in1=over_heads(COS, ROPE))
+                crossed = results.tile([P, 2, HEADS_PER_HALF, PAIRS], F32)
+                nc.vector.tensor_mul(
+                    out=crossed[:, 0], in0=pairs[:, :, :, 1], in1=over_heads(MINUS_SIN, PAIRS)
+                )
+                nc.vector.tensor_mul(
+                    out=crossed[:, 1], in0=pairs[:, :, :, 0], in1=over_heads(PLUS_SIN, PAIRS)
+                )
+                nc.vector.tensor_add(
+                    out=result[:, :, NOPE:QH].rearrange("p h (i e) -> p h i e", e=2),
+                    in0=straight[:].rearrange("p h (i e) -> p h i e", e=2),
+                    in1=crossed[:].rearrange("p e h i -> p h i e"),
+                )
+                heads = slice(half * HEADS_PER_HALF, (half + 1) * HEADS_PER_HALF)
+                nc.sync.dma_start(out=out[b, heads].rearrange("h n d -> n h d"), in_=result[:])

@@ -23,15 +23,13 @@ K_PASS = P * PACK
 BANK = 512
 
 N_GROUPS = QR // K_PASS
-SLAB = 1024
-GROUPS_PER_SLAB = SLAB // K_PASS
 HALVES = HQ // BANK
 HEADS_PER_HALF = BANK // QH
 PAIRS = ROPE // 2
 
 RUN = 4
 WQA_SCALAR_COLUMNS = 128
-RAW_BUFS = 12
+RAW_BUFS = 8
 
 ROUND_MAGIC = 1.5 * 2.0**23
 
@@ -45,7 +43,7 @@ def tile_multilatentattention_pa_k_kernel(tc, x, Wqa, Wqb, out):
         const = ctx.enter_context(tc.tile_pool(name="const", bufs=1))
         raw = ctx.enter_context(tc.tile_pool(name="raw", bufs=RAW_BUFS))
         work = ctx.enter_context(tc.tile_pool(name="work", bufs=3))
-        results = ctx.enter_context(tc.tile_pool(name="results", bufs=2))
+        results = ctx.enter_context(tc.tile_pool(name="results", bufs=B * HALVES))
         cq_psum = ctx.enter_context(tc.psum_pool(name="cq_psum", bufs=4))
         q_psum = ctx.enter_context(tc.psum_pool(name="q_psum", bufs=1))
 
@@ -77,13 +75,13 @@ def tile_multilatentattention_pa_k_kernel(tc, x, Wqa, Wqb, out):
         make_identity(nc, identity[:])
 
         turns = const.tile([P, PAIRS], F32)
-        nc.vector.tensor_scalar(
+        nc.gpsimd.tensor_scalar(
             out=turns[:, 0:1], in0=position[:], scalar1=1.0 / (2.0 * math.pi), scalar2=None, op0=ALU.mult
         )
         ratio = BASE ** (-2.0 / ROPE)
         filled = 1
         while filled < PAIRS:
-            nc.vector.tensor_scalar(
+            nc.gpsimd.tensor_scalar(
                 out=turns[:, filled : 2 * filled],
                 in0=turns[:, 0:filled],
                 scalar1=ratio**filled,
@@ -95,19 +93,19 @@ def tile_multilatentattention_pa_k_kernel(tc, x, Wqa, Wqb, out):
         MINUS_SIN = slice(ROPE, ROPE + PAIRS)
         PLUS_SIN = slice(ROPE + PAIRS, ROPE + 2 * PAIRS)
         phase = const.tile([P, ROPE + 2 * PAIRS], F32)
-        nc.vector.tensor_scalar(
+        nc.gpsimd.tensor_scalar(
             out=phase[:, COS].rearrange("p (i e) -> p i e", e=2),
             in0=turns[:].unsqueeze(2).to_broadcast([P, PAIRS, 2]),
             scalar1=0.25,
             scalar2=None,
             op0=ALU.add,
         )
-        nc.vector.tensor_scalar(
+        nc.gpsimd.tensor_scalar(
             out=phase[:, MINUS_SIN], in0=turns[:], scalar1=-1.0, scalar2=None, op0=ALU.mult
         )
-        nc.vector.tensor_copy(out=phase[:, PLUS_SIN], in_=turns[:])
+        nc.gpsimd.tensor_copy(out=phase[:, PLUS_SIN], in_=turns[:])
         whole = const.tile([P, ROPE + 2 * PAIRS], F32)
-        nc.vector.tensor_scalar(
+        nc.gpsimd.tensor_scalar(
             out=whole[:],
             in0=phase[:],
             scalar1=ROUND_MAGIC,
@@ -116,9 +114,7 @@ def tile_multilatentattention_pa_k_kernel(tc, x, Wqa, Wqb, out):
             op1=ALU.subtract,
         )
         part = const.tile([P, ROPE + 2 * PAIRS], F32)
-        nc.vector.tensor_sub(out=part[:], in0=phase[:], in1=whole[:])
-        table = const.tile([P, ROPE + 2 * PAIRS], F32)
-        nc.scalar.activation(out=table[:], in_=part[:], func=ACT.Sin, scale=2.0 * math.pi)
+        nc.gpsimd.tensor_tensor(out=part[:], in0=phase[:], in1=whole[:], op=ALU.subtract)
 
         x_pairs = x_rows[:].bitcast(F32).rearrange("n b (p u) -> n b u p", u=2)
         x_turned = cq_psum.tile([P, PACK, P], F32, name="x_turned", tag="cq_bank")
@@ -142,19 +138,16 @@ def tile_multilatentattention_pa_k_kernel(tc, x, Wqa, Wqb, out):
                 q_sums[(b, half)] = q_psum.tile(
                     [P, BANK], F32, name="q_sums_%d_%d" % (b, half), tag="q_sums_%d_%d" % (b, half)
                 )
-        wqa_rows, wqa_grouped, wqa_words, wqa_scales = {}, {}, {}, {}
+        wqa_grouped, wqa_words, wqa_scales = {}, {}, {}
         cq_banks, cq_grouped = {}, {}
         wqb_grouped, wqb_words, wqb_scales = {}, {}, {}
 
         def regroup_wqa(g):
-            slab, place = divmod(g, GROUPS_PER_SLAB)
-            if place == 0:
-                wqa_rows[slab] = raw.tile([P, PACK, SLAB], BF16, name="wqa_rows", tag="rows")
-                nc.sync.dma_start(
-                    out=wqa_rows[slab][:],
-                    in_=Wqa[:, slab * SLAB : (slab + 1) * SLAB].rearrange("(p t) w -> p t w", t=PACK),
-                )
-            rows = wqa_rows[slab][:, :, place * K_PASS : (place + 1) * K_PASS]
+            rows = raw.tile([P, PACK, K_PASS], BF16, name="wqa_rows", tag="wqa_rows")
+            nc.sync.dma_start(
+                out=rows[:],
+                in_=Wqa[:, g * K_PASS : (g + 1) * K_PASS].rearrange("(p t) w -> p t w", t=PACK),
+            )
             wqa_grouped[g] = work.tile(
                 [P, K_PASS, PACK], BF16, name="wqa_grouped", tag="wqa_grouped", align_bytes=64
             )
@@ -195,7 +188,7 @@ def tile_multilatentattention_pa_k_kernel(tc, x, Wqa, Wqb, out):
             quantise(cq_words[:, g, :], cq_scales[:, g, :], cq_grouped[g][:])
 
         def regroup_wqb(g):
-            rows = raw.tile([P, PACK, HQ], BF16, name="wqb_rows", tag="rows")
+            rows = raw.tile([P, PACK, HQ], BF16, name="wqb_rows", tag="wqb_rows")
             nc.sync.dma_start(
                 out=rows[:],
                 in_=Wqb[g * K_PASS : (g + 1) * K_PASS, :].rearrange("(t p) w -> p t w", p=P),
@@ -242,6 +235,9 @@ def tile_multilatentattention_pa_k_kernel(tc, x, Wqa, Wqb, out):
             run(round_cq, step - 2)
             run(quantise_cq, step - 3)
             run(second_product, step - N_GROUPS - 1)
+
+        table = const.tile([P, ROPE + 2 * PAIRS], F32)
+        nc.scalar.activation(out=table[:], in_=part[:], func=ACT.Sin, scale=2.0 * math.pi)
 
         def over_heads(part_of_table, width):
             return table[:, part_of_table].unsqueeze(1).to_broadcast([P, HEADS_PER_HALF, width])

@@ -116,20 +116,6 @@ def tile_multilatentattention_pa_k_kernel(tc, x, Wqa, Wqb, out):
         part = const.tile([P, ROPE + 2 * PAIRS], F32)
         nc.gpsimd.tensor_tensor(out=part[:], in0=phase[:], in1=whole[:], op=ALU.subtract)
 
-        x_pairs = x_rows[:].bitcast(F32).rearrange("n b (p u) -> n b u p", u=2)
-        x_turned = cq_psum.tile([P, PACK, P], F32, name="x_turned", tag="cq_bank")
-        for b in range(B):
-            for u in range(2):
-                nc.tensor.transpose(x_turned[:, 2 * b + u, :], x_pairs[:, b, u, :], identity[:])
-        x_grouped = const.tile([P, B * N, PACK], BF16, align_bytes=64)
-        nc.vector.tensor_copy(
-            out=x_grouped[:].bitcast(F32).rearrange("p (b n) u -> p b n u", b=B),
-            in_=x_turned[:].rearrange("p (b u) n -> p b n u", u=2),
-        )
-        x_words = const.tile([P, B * N], U32, align_bytes=64)
-        x_scales = const.tile([P, B * N], U8, align_bytes=64)
-        quantise(x_words[:], x_scales[:], x_grouped[:])
-
         cq_words = const.tile([P, N_GROUPS, B * N], U32, align_bytes=64)
         cq_scales = const.tile([P, N_GROUPS, B * N], U8, align_bytes=64)
         q_sums = {}
@@ -227,13 +213,28 @@ def tile_multilatentattention_pa_k_kernel(tc, x, Wqa, Wqb, out):
             if 0 <= g < N_GROUPS:
                 stage(g)
 
-        for step in range(2 * N_GROUPS + 1):
+        x_pairs = x_rows[:].bitcast(F32).rearrange("n b (p u) -> n b u p", u=2)
+        x_turned = cq_psum.tile([P, PACK, P], F32, name="x_turned", tag="cq_bank")
+        for b in range(B):
+            for u in range(2):
+                nc.tensor.transpose(x_turned[:, 2 * b + u, :], x_pairs[:, b, u, :], identity[:])
+        x_grouped = const.tile([P, B * N, PACK], BF16, align_bytes=64)
+        nc.scalar.copy(
+            out=x_grouped[:].bitcast(F32).rearrange("p (b n) u -> p b n u", b=B),
+            in_=x_turned[:].rearrange("p (b u) n -> p b n u", u=2),
+        )
+        x_words = const.tile([P, B * N], U32, align_bytes=64)
+        x_scales = const.tile([P, B * N], U8, align_bytes=64)
+
+        regroup_wqa(0)
+        quantise(x_words[:], x_scales[:], x_grouped[:])
+        for step in range(1, 2 * N_GROUPS + 1):
             run(regroup_wqa, step)
-            run(regroup_wqb, step - N_GROUPS)
             run(quantise_wqa, step - 1)
             run(first_product, step - 1)
             run(round_cq, step - 2)
             run(quantise_cq, step - 3)
+            run(regroup_wqb, step - N_GROUPS)
             run(second_product, step - N_GROUPS - 1)
 
         table = const.tile([P, ROPE + 2 * PAIRS], F32)
@@ -248,7 +249,6 @@ def tile_multilatentattention_pa_k_kernel(tc, x, Wqa, Wqb, out):
                 rotated = q[:, :, NOPE:QH]
                 pairs = rotated.rearrange("p h (i e) -> p h i e", e=2)
                 result = results.tile([P, HEADS_PER_HALF, QH], F32)
-                nc.scalar.copy(out=result[:, :, 0:NOPE], in_=q[:, :, 0:NOPE])
                 straight = results.tile([P, HEADS_PER_HALF, ROPE], F32)
                 nc.vector.tensor_mul(out=straight[:], in0=rotated, in1=over_heads(COS, ROPE))
                 crossed = results.tile([P, 2, HEADS_PER_HALF, PAIRS], F32)
@@ -258,6 +258,7 @@ def tile_multilatentattention_pa_k_kernel(tc, x, Wqa, Wqb, out):
                 nc.vector.tensor_mul(
                     out=crossed[:, 1], in0=pairs[:, :, :, 0], in1=over_heads(PLUS_SIN, PAIRS)
                 )
+                nc.scalar.copy(out=result[:, :, 0:NOPE], in_=q[:, :, 0:NOPE])
                 nc.vector.tensor_add(
                     out=result[:, :, NOPE:QH].rearrange("p h (i e) -> p h i e", e=2),
                     in0=straight[:].rearrange("p h (i e) -> p h i e", e=2),

import math
from contextlib import ExitStack

import concourse.mybir as mybir
from concourse.masks import make_identity

F32 = mybir.dt.float32
BF16 = mybir.dt.bfloat16
U32 = mybir.dt.uint32
U8 = mybir.dt.uint8
FP8X4 = mybir.dt.float8_e4m3fn_x4
ALU = mybir.AluOpType
ACT = mybir.ActivationFunctionType

B, N, E, H, NOPE, ROPE, QR = 2, 128, 512, 16, 32, 32, 8192
QH = NOPE + ROPE
HQ = H * QH
BASE = 10000.0

P = 128
PACK = 4
K_PASS = P * PACK
BANK = 512

N_GROUPS = QR // K_PASS
HALVES = HQ // BANK
HEADS_PER_HALF = BANK // QH
PAIRS = ROPE // 2

RUN = 4
WQA_SCALAR_COLUMNS = 128
RAW_BUFS = 8

ROUND_MAGIC = 1.5 * 2.0**23

FLOPS = 2 * B * N * E * QR + 2 * B * N * QR * HQ


def tile_multilatentattention_pa_k_kernel(tc, x, Wqa, Wqb, out):
    nc = tc.nc
    with ExitStack() as ctx:
        ctx.enter_context(tc.manual_schedule())
        const = ctx.enter_context(tc.tile_pool(name="const", bufs=1))
        raw = ctx.enter_context(tc.tile_pool(name="raw", bufs=RAW_BUFS))
        work = ctx.enter_context(tc.tile_pool(name="work", bufs=3))
        results = ctx.enter_context(tc.tile_pool(name="results", bufs=B * HALVES))
        cq_psum = ctx.enter_context(tc.psum_pool(name="cq_psum", bufs=4))
        q_psum = ctx.enter_context(tc.psum_pool(name="q_psum", bufs=1))

        def regroup(copy, grouped, rows):
            copy(
                out=grouped.rearrange("p (c i) t -> p c t i", i=RUN),
                in_=rows.rearrange("p t (c i) -> p c t i", i=RUN),
            )

        def quantise(words, scales, grouped):
            nc.vector.quantize_mx(
                out=words.bitcast(FP8X4),
                scales=scales,
                in_=grouped.rearrange("p w t -> p (w t)"),
            )

        x_rows = const.tile([P, B, E], BF16)
        nc.sync.dma_start(out=x_rows[:], in_=x.rearrange("b n e -> n b e"))

        position = const.tile([P, 1], F32)
        nc.gpsimd.iota(
            position[:],
            pattern=[[0, 1]],
            base=0,
            channel_multiplier=1,
            allow_small_or_imprecise_dtypes=True,
        )
        identity = const.tile([P, P], F32)
        make_identity(nc, identity[:])

        turns = const.tile([P, PAIRS], F32)
        nc.gpsimd.tensor_scalar(
            out=turns[:, 0:1], in0=position[:], scalar1=1.0 / (2.0 * math.pi), scalar2=None, op0=ALU.mult
        )
        ratio = BASE ** (-2.0 / ROPE)
        filled = 1
        while filled < PAIRS:
            nc.gpsimd.tensor_scalar(
                out=turns[:, filled : 2 * filled],
                in0=turns[:, 0:filled],
                scalar1=ratio**filled,
                scalar2=None,
                op0=ALU.mult,
            )
            filled *= 2
        COS = slice(0, ROPE)
        MINUS_SIN = slice(ROPE, ROPE + PAIRS)
        PLUS_SIN = slice(ROPE + PAIRS, ROPE + 2 * PAIRS)
        phase = const.tile([P, ROPE + 2 * PAIRS], F32)
        nc.gpsimd.tensor_scalar(
            out=phase[:, COS].rearrange("p (i e) -> p i e", e=2),
            in0=turns[:].unsqueeze(2).to_broadcast([P, PAIRS, 2]),
            scalar1=0.25,
            scalar2=None,
            op0=ALU.add,
        )
        nc.gpsimd.tensor_scalar(
            out=phase[:, MINUS_SIN], in0=turns[:], scalar1=-1.0, scalar2=None, op0=ALU.mult
        )
        nc.gpsimd.tensor_copy(out=phase[:, PLUS_SIN], in_=turns[:])
        whole = const.tile([P, ROPE + 2 * PAIRS], F32)
        nc.gpsimd.tensor_scalar(
            out=whole[:],
            in0=phase[:],
            scalar1=ROUND_MAGIC,
            scalar2=ROUND_MAGIC,
            op0=ALU.add,
            op1=ALU.subtract,
        )
        part = const.tile([P, ROPE + 2 * PAIRS], F32)
        nc.gpsimd.tensor_tensor(out=part[:], in0=phase[:], in1=whole[:], op=ALU.subtract)

        cq_words = const.tile([P, N_GROUPS, B * N], U32, align_bytes=64)
        cq_scales = const.tile([P, N_GROUPS, B * N], U8, align_bytes=64)
        q_sums = {}
        for b in range(B):
            for half in range(HALVES):
                q_sums[(b, half)] = q_psum.tile(
                    [P, BANK], F32, name="q_sums_%d_%d" % (b, half), tag="q_sums_%d_%d" % (b, half)
                )
        wqa_grouped, wqa_words, wqa_scales = {}, {}, {}
        cq_banks, cq_grouped = {}, {}
        wqb_grouped, wqb_words, wqb_scales = {}, {}, {}

        def regroup_wqa(g):
            rows = raw.tile([P, PACK, K_PASS], BF16, name="wqa_rows", tag="wqa_rows")
            nc.sync.dma_start(
                out=rows[:],
                in_=Wqa[:, g * K_PASS : (g + 1) * K_PASS].rearrange("(p t) w -> p t w", t=PACK),
            )
            wqa_grouped[g] = work.tile(
                [P, K_PASS, PACK], BF16, name="wqa_grouped", tag="wqa_grouped", align_bytes=64
            )
            cut = WQA_SCALAR_COLUMNS
            regroup(nc.scalar.copy, wqa_grouped[g][:, 0:cut, :], rows[:, :, 0:cut])
            regroup(nc.vector.tensor_copy, wqa_grouped[g][:, cut:K_PASS, :], rows[:, :, cut:K_PASS])

        def quantise_wqa(g):
            wqa_words[g] = work.tile([P, K_PASS], U32, name="wqa_words", tag="wqa_words", align_bytes=64)
            wqa_scales[g] = work.tile([P, K_PASS], U8, name="wqa_scales", tag="wqa_scales", align_bytes=64)
            quantise(wqa_words[g][:], wqa_scales[g][:], wqa_grouped[g][:])

        def first_product(g):
            for b in range(B):
                cq_banks[(g, b)] = cq_psum.tile([P, PACK, N], F32, name="cq_bank", tag="cq_bank")
                for t in range(PACK):
                    nc.tensor.matmul_mx(
                        out=cq_banks[(g, b)][:, t, :],
                        lhsT=wqa_words[g][:, t * P : (t + 1) * P].bitcast(FP8X4),
                        lhsT_scale=wqa_scales[g][:, t * P : (t + 1) * P],
                        rhs=x_words[:, b * N : (b + 1) * N].bitcast(FP8X4),
                        rhs_scale=x_scales[:, b * N : (b + 1) * N],
                        start=True,
                        stop=True,
                    )

        def round_cq(g):
            cq_grouped[g] = work.tile(
                [P, B * N, PACK], BF16, name="cq_grouped", tag="cq_grouped", align_bytes=64
            )
            for b in range(B):
                nc.scalar.copy(
                    out=cq_grouped[g][:, b * N : (b + 1) * N, :],
                    in_=cq_banks[(g, b)][:].rearrange("p t n -> p n t"),
                )

        def quantise_cq(g):
            quantise(cq_words[:, g, :], cq_scales[:, g, :], cq_grouped[g][:])

        def regroup_wqb(g):
            rows = raw.tile([P, PACK, HQ], BF16, name="wqb_rows", tag="wqb_rows")
            nc.sync.dma_start(
                out=rows[:],
                in_=Wqb[g * K_PASS : (g + 1) * K_PASS, :].rearrange("(t p) w -> p t w", p=P),
            )
            for half, copy in enumerate((nc.scalar.copy, nc.vector.tensor_copy)):
                wqb_grouped[(g, half)] = work.tile(
                    [P, BANK, PACK],
                    BF16,
                    name="wqb_grouped_%d" % half,
                    tag="wqb_grouped_%d" % half,
                    align_bytes=64,
                )
                regroup(copy, wqb_grouped[(g, half)][:], rows[:, :, half * BANK : (half + 1) * BANK])

        def second_product(g):
            for half in range(HALVES):
                wqb_words[half] = work.tile(
                    [P, BANK], U32, name="wqb_words_%d" % half, tag="wqb_words_%d" % half, align_bytes=64
                )
                wqb_scales[half] = work.tile(
                    [P, BANK], U8, name="wqb_scales_%d" % half, tag="wqb_scales_%d" % half, align_bytes=64
                )
                quantise(wqb_words[half][:], wqb_scales[half][:], wqb_grouped[(g, half)][:])
                for b in range(B):
                    nc.tensor.matmul_mx(
                        out=q_sums[(b, half)][:],
                        lhsT=cq_words[:, g, b * N : (b + 1) * N].bitcast(FP8X4),
                        lhsT_scale=cq_scales[:, g, b * N : (b + 1) * N],
                        rhs=wqb_words[half][:].bitcast(FP8X4),
                        rhs_scale=wqb_scales[half][:],
                        start=(g == 0),
                        stop=(g == N_GROUPS - 1),
                    )

        def run(stage, g):
            if 0 <= g < N_GROUPS:
                stage(g)

        x_pairs = x_rows[:].bitcast(F32).rearrange("n b (p u) -> n b u p", u=2)
        x_turned = cq_psum.tile([P, PACK, P], F32, name="x_turned", tag="cq_bank")
        for b in range(B):
            for u in range(2):
                nc.tensor.transpose(x_turned[:, 2 * b + u, :], x_pairs[:, b, u, :], identity[:])
        x_grouped = const.tile([P, B * N, PACK], BF16, align_bytes=64)
        nc.scalar.copy(
            out=x_grouped[:].bitcast(F32).rearrange("p (b n) u -> p b n u", b=B),
            in_=x_turned[:].rearrange("p (b u) n -> p b n u", u=2),
        )
        x_words = const.tile([P, B * N], U32, align_bytes=64)
        x_scales = const.tile([P, B * N], U8, align_bytes=64)

        regroup_wqa(0)
        quantise(x_words[:], x_scales[:], x_grouped[:])
        for step in range(1, 2 * N_GROUPS + 1):
            run(regroup_wqa, step)
            run(quantise_wqa, step - 1)
            run(first_product, step - 1)
            run(round_cq, step - 2)
            run(quantise_cq, step - 3)
            run(regroup_wqb, step - N_GROUPS)
            run(second_product, step - N_GROUPS - 1)

        table = const.tile([P, ROPE + 2 * PAIRS], F32)
        nc.scalar.activation(out=table[:], in_=part[:], func=ACT.Sin, scale=2.0 * math.pi)

        def over_heads(part_of_table, width):
            return table[:, part_of_table].unsqueeze(1).to_broadcast([P, HEADS_PER_HALF, width])

        for half in range(HALVES):
            for b in range(B):
                q = q_sums[(b, half)][:].rearrange("p (h d) -> p h d", d=QH)
                rotated = q[:, :, NOPE:QH]
                pairs = rotated.rearrange("p h (i e) -> p h i e", e=2)
                result = results.tile([P, HEADS_PER_HALF, QH], F32)
                straight = results.tile([P, HEADS_PER_HALF, ROPE], F32)
                nc.vector.tensor_mul(out=straight[:], in0=rotated, in1=over_heads(COS, ROPE))
                crossed = results.tile([P, 2, HEADS_PER_HALF, PAIRS], F32)
                nc.vector.tensor_mul(
                    out=crossed[:, 0], in0=pairs[:, :, :, 1], in1=over_heads(MINUS_SIN, PAIRS)
                )
                nc.vector.tensor_mul(
                    out=crossed[:, 1], in0=pairs[:, :, :, 0], in1=over_heads(PLUS_SIN, PAIRS)
                )
                nc.scalar.copy(out=result[:, :, 0:NOPE], in_=q[:, :, 0:NOPE])
                nc.vector.tensor_add(
                    out=result[:, :, NOPE:QH].rearrange("p h (i e) -> p h i e", e=2),
                    in0=straight[:].rearrange("p h (i e) -> p h i e", e=2),
                    in1=crossed[:].rearrange("p e h i -> p h i e"),
                )
                heads = slice(half * HEADS_PER_HALF, (half + 1) * HEADS_PER_HALF)
                nc.sync.dma_start(out=out[b, heads].rearrange("h n d -> n h d"), in_=result[:])
